import numpy as np
import ml_dtypes


BF16 = ml_dtypes.bfloat16


def bf(x):
    return np.asarray(x, np.float32).astype(BF16)


def f64(x):
    return np.asarray(x).astype(np.float64)


E2M1 = np.array([0.0, 0.5, 1.0, 1.5, 2.0, 3.0, 4.0, 6.0, -0.0, -0.5, -1.0, -1.5, -2.0, -3.0, -4.0, -6.0])


def pack_weight(w, fmt):
    k, n = w.shape
    w = f64(bf(w)).reshape(k // 32, 32, n)
    amax = np.abs(w).max(1)
    if fmt == "e4m3":
        byte = np.frexp(amax)[1] - 1 + 127 - 7
    else:
        mant, ex = np.frexp(amax / 6.0)
        byte = np.where(mant > 0.5, ex, ex - 1) + 127
    byte = np.clip(np.where(amax > 0, byte, 1), 1, 254)
    scaled = (w * np.exp2(127.0 - byte)[:, None, :]).reshape(k, n).astype(np.float32)
    by_word = np.ascontiguousarray(scaled.reshape(k // 512, 128, 4, n).transpose(0, 1, 3, 2))
    if fmt == "e4m3":
        words = by_word.astype(ml_dtypes.float8_e4m3fn).view(np.uint8)
    else:
        c = by_word.astype(ml_dtypes.float4_e2m1fn).view(np.uint8) & 0xF
        words = c[..., 0::2] | (c[..., 1::2] << 4)
    return np.ascontiguousarray(words), np.ascontiguousarray(byte.astype(np.uint8).reshape(k // 512, 16, n))


def unpack_weight(words, scales, fmt):
    g, p, n, _ = words.shape
    if fmt == "e4m3":
        vals = np.ascontiguousarray(words).view(ml_dtypes.float8_e4m3fn).astype(np.float64)
    else:
        nib = np.empty((g, p, n, 4), np.uint8)
        nib[..., 0::2] = words & 0xF
        nib[..., 1::2] = words >> 4
        vals = E2M1[nib]
    vals = vals * np.repeat(np.exp2(scales.astype(np.float64) - 127.0), 8, axis=1)[..., None]
    return vals.transpose(0, 1, 3, 2).reshape(g * 512, n)

def pack4(w):
    words, scales = pack_weight(w, "e2m1")
    return words.reshape(words.shape[0], 128, -1), scales


def unpack4(words, scales):
    return unpack_weight(words.reshape(words.shape[0], 128, -1, 2), scales, "e2m1")


def kspread(k):
    return np.exp2(np.repeat(np.random.randint(-6, 7, k // 32), 32).astype(np.float64))


B, T, E, V, H, C = 1, 1024, 1536, 3072, 8, 512
KD = E // H
ROPE_BASE = 10000.0


def rotate_every_two(u):
    u1 = u[..., ::2]
    u2 = u[..., 1::2]
    return np.stack((-u2, u1), axis=-1).reshape(u.shape)


def theta_shift(u, sin, cos):
    return u * cos + rotate_every_two(u) * sin


def setup_inputs():
    s = kspread(E)
    angle = np.arange(T)[:, None] * (1.0 / ROPE_BASE ** (np.repeat(np.arange(KD // 2), 2) * 2.0 / KD))
    x = np.random.standard_normal((B, T, E)) * s
    x_words, x_scales = pack4(x.reshape(B * T, E).T)
    sin = bf(np.sin(angle))
    cos = bf(np.cos(angle))
    Wq_words, Wq_scales = pack4(np.random.standard_normal((E, E)) * 0.5 / np.sqrt(E) / s[:, None])
    Wk_words, Wk_scales = pack4(np.random.standard_normal((E, E)) * 2.0 / np.sqrt(E) / s[:, None])
    return {"x_words": x_words, "x_scales": x_scales,
            "sin": sin, "cos": cos,
            "Wq_words": Wq_words, "Wq_scales": Wq_scales,
            "Wk_words": Wk_words, "Wk_scales": Wk_scales}


def reference(x_words, x_scales, sin, cos, Wq_words, Wq_scales, Wk_words, Wk_scales):
    xq = unpack4(x_words, x_scales).T.reshape(B, T, E)
    q = (xq @ unpack4(Wq_words, Wq_scales)).reshape(B, T, H, KD).transpose(0, 2, 1, 3)
    k = ((xq @ unpack4(Wk_words, Wk_scales)) * KD ** -0.5).reshape(B, T, H, KD).transpose(0, 2, 1, 3)
    return theta_shift(q, f64(sin), f64(cos)), theta_shift(k, f64(sin), f64(cos))

@@ -1,0 +1,221 @@
+from contextlib import ExitStack
+
+import concourse.mybir as mybir
+
+F32 = mybir.dt.float32
+BF16 = mybir.dt.bfloat16
+I32 = mybir.dt.int32
+U8 = mybir.dt.uint8
+FP4X4 = mybir.dt.float4_e2m1fn_x4
+COPY = mybir.ActivationFunctionType.Copy
+MULT = mybir.AluOpType.mult
+ADD = mybir.AluOpType.add
+
+P = 128
+T, E, H, KD = 1024, 1536, 8, 192
+G = E // 512
+TT = T // P
+BH = 2
+BC = BH * KD
+NB = H // BH
+K_SCALE = KD ** -0.5
+NS = 40
+V_UNITS = (13, 14, 15)
+
+FLOPS = 2 * T * E * (2 * E) + 3 * T * 2 * E
+
+
+def pairs(ap, swap):
+    v = ap.rearrange("p h (i two) -> p h i two", two=2)
+    return v[:, :, :, ::-1] if swap else v
+
+
+def tile_multiscaleretention_pa_kernel(tc, x_words, x_scales, sin, cos, Wq_words, Wq_scales, Wk_words, Wk_scales, out_0, out_1):
+    nc = tc.nc
+    outs = (out_0, out_1)
+    with ExitStack() as ctx:
+        keep = ctx.enter_context(tc.tile_pool(name="keep", bufs=1))
+        prods = ctx.enter_context(tc.tile_pool(name="prods", bufs=8))
+        results = ctx.enter_context(tc.tile_pool(name="results", bufs=8))
+        heads = ctx.enter_context(tc.tile_pool(name="heads", bufs=2))
+        psum = ctx.enter_context(tc.psum_pool(name="psum", bufs=8))
+        ctx.enter_context(tc.manual_schedule())
+
+        def codes_tile(name, cols):
+            return keep.tile([P, G, 2 * cols], U8, name=name, align_bytes=64)
+
+        def plane_tile(name, cols):
+            plane = keep.tile([P, G, cols], U8, name=name, align_bytes=64)
+            nc.vector.memset(plane[:].rearrange("p g n -> p (g n)").bitcast(I32), 0)
+            return plane
+
+        def load_codes(tile, words, c0, cols):
+            nc.sync.dma_start(out=tile[:].bitcast(I32), in_=words[:, :, 2 * c0 : 2 * (c0 + cols)].rearrange("g p n -> p g n").bitcast(I32))
+
+        def load_plane(tile, scales, c0, cols):
+            for q in range(4):
+                nc.sync.dma_start(
+                    out=tile[32 * q : 32 * q + 4, :, :].bitcast(I32),
+                    in_=scales[:, 4 * q : 4 * q + 4, c0 : c0 + cols].rearrange("g r n -> r g n").bitcast(I32),
+                )
+
+        tab = keep.tile([P, TT, 2, KD], BF16, name="tab")
+        sraw = keep.tile([P, TT, KD], BF16, name="sraw")
+        sgn = keep.tile([P, 2], BF16, name="sgn")
+        nc.gpsimd.dma_start(out=sraw[:], in_=sin.rearrange("(t p) c -> p t c", p=P))
+        nc.gpsimd.dma_start(out=tab[:, :, 0, :], in_=cos.rearrange("(t p) c -> p t c", p=P))
+        nc.gpsimd.memset(sgn[:, 0:1], 1.0)
+        nc.gpsimd.memset(sgn[:, 1:2], -1.0)
+
+        xs = plane_tile("xs", T)
+        wqs_a = plane_tile("wqs_a", 2 * BC)
+        wqs_b = plane_tile("wqs_b", 2 * BC)
+        wks = plane_tile("wks", E)
+        x0 = codes_tile("x0", P)
+        xr = codes_tile("xr", T - P)
+        wq_a = codes_tile("wq_a", BC)
+        wq_b = codes_tile("wq_b", E - BC)
+        wk = codes_tile("wk", E)
+        load_codes(x0, x_words, 0, P)
+        load_codes(wq_a, Wq_words, 0, BC)
+        load_plane(xs, x_scales, 0, T)
+        load_plane(wqs_a, Wq_scales, 0, 2 * BC)
+        load_codes(wq_b, Wq_words, BC, E - BC)
+        load_plane(wqs_b, Wq_scales, 2 * BC, 2 * BC)
+        load_codes(wk, Wk_words, 0, E)
+        load_plane(wks, Wk_scales, 0, E)
+        load_codes(xr, x_words, P, T - P)
+
+        sgn_b = sgn[:].unsqueeze(1)
+        for t0, t1 in ((0, 1), (1, TT)):
+            nc.gpsimd.tensor_tensor(
+                out=pairs(tab[:, t0:t1, 1, :], False),
+                in0=pairs(sraw[:, t0:t1, :], True),
+                in1=sgn_b.unsqueeze(1).to_broadcast([P, t1 - t0, KD // 2, 2]),
+                op=MULT,
+            )
+        tabk = keep.tile([P, TT, 2, KD], F32, name="tabk")
+        tabf = keep.tile([P, TT * 2, NS], F32, name="tabf")
+
+        def scale_table(t0, t1):
+            nc.scalar.activation(
+                out=tabk[:, t0:t1].rearrange("p t a c -> p (t a c)"),
+                in_=tab[:, t0:t1].rearrange("p t a c -> p (t a c)"),
+                func=COPY,
+                scale=K_SCALE,
+            )
+
+        scale_table(0, 1)
+
+        def x_of(t):
+            return (x0, 0) if t == 0 else (xr, (t - 1) * P)
+
+        def w_codes(qk, c):
+            if qk:
+                return wk, c
+            return (wq_a, c) if c < BC else (wq_b, c - BC)
+
+        def w_plane(qk, c):
+            if qk:
+                return wks, c
+            return (wqs_a, c) if c < 2 * BC else (wqs_b, c - 2 * BC)
+
+        def multiply(t, qk, b):
+            ps = psum.tile([P, BC], F32, name="ps")
+            xt, xc = x_of(t)
+            for n0, n in ((0, 256), (256, 128)):
+                c = b * BC + n0
+                wt, wc = w_codes(qk, c)
+                st, sc = w_plane(qk, c)
+                for g in range(G):
+                    nc.tensor.matmul_mx(
+                        out=ps[:, n0 : n0 + n],
+                        lhsT=xt[:, g, 2 * xc : 2 * (xc + P)].bitcast(FP4X4),
+                        lhsT_scale=xs[:, g, t * P : (t + 1) * P],
+                        rhs=wt[:, g, 2 * wc : 2 * (wc + n)].bitcast(FP4X4),
+                        rhs_scale=st[:, g, sc : sc + n],
+                        start=(g == 0),
+                        stop=(g == G - 1),
+                    )
+            return ps[:].rearrange("p (h c) -> p h c", h=BH)
+
+        def add(engine, m, res, h0, h1, ns):
+            engine.tensor_tensor(
+                out=pairs(res[:, h0:h1, ns:], False),
+                in0=pairs(m[:, h0:h1, 0, :], False),
+                in1=pairs(m[:, h0:h1, 1, :], True),
+                op=ADD,
+            )
+
+        def add_s(engine, ms, res, qk):
+            v = ms[:, :, :, qk * H : (qk + 1) * H].rearrange("p a c h -> p a h c")
+            engine.tensor_tensor(
+                out=pairs(res[:, :, 0:NS], False), in0=pairs(v[:, 0], False), in1=pairs(v[:, 1], True), op=ADD
+            )
+
+        def store(t, qk, res, h0, h1):
+            nc.sync.dma_start(
+                out=outs[qk][0, h0:h1, t * P : (t + 1) * P, :].rearrange("h t c -> t h c"), in_=res[:, h0:h1, :]
+            )
+
+        ms_of = {}
+        uc_of = {}
+        m_of = {}
+        res_of = {}
+        for t in range(TT):
+            ns = NS if t < TT - 1 else 0
+            w = KD - ns
+            if ns:
+                uc = heads.tile([P, 2 * H, NS], F32, name="uc")
+                uc_of[t] = uc
+            if t and NS:
+                ms = heads.tile([P, 2, NS, 2 * H], F32, name="ms")
+                ms_of[t - 1] = ms
+            for qk in range(2):
+                m = prods.tile([P, H, 2, w], F32, name="m")
+                res = results.tile([P, H, KD], F32, name="res")
+                m_of[t, qk] = m
+                res_of[t, qk] = res
+                for b in range(NB):
+                    u = multiply(t, qk, b)
+                    hs = slice(BH * b, BH * (b + 1))
+                    if ns:
+                        dst = uc_of[t][:, qk * H + BH * b : qk * H + BH * (b + 1), :]
+                        if qk:
+                            nc.scalar.activation(out=dst, in_=u[:, :, 0:NS], func=COPY, scale=K_SCALE)
+                        else:
+                            nc.scalar.copy(out=dst, in_=u[:, :, 0:NS])
+                    if t and NS:
+                        i = qk * NB + b
+                        for j in range(2 * NS * i // 8, 2 * NS * (i + 1) // 8):
+                            c, a = divmod(j, 2)
+                            k = 2 * (t - 1) + a
+                            nc.scalar.activation(
+                                out=ms_of[t - 1][:, a, c, :], in_=uc_of[t - 1][:, :, c], func=COPY, scale=tabf[:, k, c : c + 1]
+                            )
+                    shape = [P, BH, 2, w]
+                    in0 = u[:, :, ns:].unsqueeze(2).to_broadcast(shape)
+                    in1 = (tabk if qk else tab)[:, t, :, ns:].unsqueeze(1).to_broadcast(shape)
+                    nc.vector.tensor_tensor(out=m[:, hs], in0=in0, in1=in1, op=MULT)
+                    if t == 0 and qk == 0:
+                        add(nc.gpsimd, m, res, BH * b, BH * (b + 1), ns)
+                    elif (2 * t + qk) not in V_UNITS and b % 2:
+                        add(nc.gpsimd, m, res, BH * (b - 1), BH * (b + 1), ns)
+            if t == 0:
+                nc.scalar.copy(out=tabf[:], in_=tab[:].rearrange("p t a c -> p (t a) c")[:, :, 0:NS])
+                scale_table(1, TT)
+            if t:
+                for qk in range(2):
+                    if NS:
+                        add_s(nc.gpsimd, ms_of[t - 1], res_of[t - 1, qk], qk)
+                    if 2 * (t - 1) + qk not in V_UNITS:
+                        store(t - 1, qk, res_of[t - 1, qk], 0, H)
+        for u in range(2 * (TT - 1), 2 * TT):
+            if u not in V_UNITS:
+                store(u // 2, u % 2, res_of[divmod(u, 2)], 0, H)
+        for u in V_UNITS:
+            t, qk = divmod(u, 2)
+            ns = NS if t < TT - 1 else 0
+            for h0 in (0, H // 2):
+                add(nc.vector, m_of[t, qk], res_of[t, qk], h0, h0 + H // 2, ns)
+                store(t, qk, res_of[t, qk], h0, h0 + H // 2)

@@ -19,7 +19,7 @@ BH = 2
 BC = BH * KD
 NB = H // BH
 K_SCALE = KD ** -0.5
-NS = 40
+NS = 0
 V_UNITS = (13, 14, 15)
 
 FLOPS = 2 * T * E * (2 * E) + 3 * T * 2 * E
@@ -37,7 +37,6 @@ def tile_multiscaleretention_pa_kernel(tc, x_words, x_scales, sin, cos, Wq_words
         keep = ctx.enter_context(tc.tile_pool(name="keep", bufs=1))
         prods = ctx.enter_context(tc.tile_pool(name="prods", bufs=8))
         results = ctx.enter_context(tc.tile_pool(name="results", bufs=8))
-        heads = ctx.enter_context(tc.tile_pool(name="heads", bufs=2))
         psum = ctx.enter_context(tc.psum_pool(name="psum", bufs=8))
         ctx.enter_context(tc.manual_schedule())
 
@@ -95,7 +94,6 @@ def tile_multiscaleretention_pa_kernel(tc, x_words, x_scales, sin, cos, Wq_words
                 op=MULT,
             )
         tabk = keep.tile([P, TT, 2, KD], F32, name="tabk")
-        tabf = keep.tile([P, TT * 2, NS], F32, name="tabf")
 
         def scale_table(t0, t1):
             nc.scalar.activation(
@@ -147,30 +145,17 @@ def tile_multiscaleretention_pa_kernel(tc, x_words, x_scales, sin, cos, Wq_words
                 op=ADD,
             )
 
-        def add_s(engine, ms, res, qk):
-            v = ms[:, :, :, qk * H : (qk + 1) * H].rearrange("p a c h -> p a h c")
-            engine.tensor_tensor(
-                out=pairs(res[:, :, 0:NS], False), in0=pairs(v[:, 0], False), in1=pairs(v[:, 1], True), op=ADD
-            )
 
         def store(t, qk, res, h0, h1):
             nc.sync.dma_start(
                 out=outs[qk][0, h0:h1, t * P : (t + 1) * P, :].rearrange("h t c -> t h c"), in_=res[:, h0:h1, :]
             )
 
-        ms_of = {}
-        uc_of = {}
         m_of = {}
         res_of = {}
         for t in range(TT):
             ns = NS if t < TT - 1 else 0
             w = KD - ns
-            if ns:
-                uc = heads.tile([P, 2 * H, NS], F32, name="uc")
-                uc_of[t] = uc
-            if t and NS:
-                ms = heads.tile([P, 2, NS, 2 * H], F32, name="ms")
-                ms_of[t - 1] = ms
             for qk in range(2):
                 m = prods.tile([P, H, 2, w], F32, name="m")
                 res = results.tile([P, H, KD], F32, name="res")
@@ -179,20 +164,6 @@ def tile_multiscaleretention_pa_kernel(tc, x_words, x_scales, sin, cos, Wq_words
                 for b in range(NB):
                     u = multiply(t, qk, b)
                     hs = slice(BH * b, BH * (b + 1))
-                    if ns:
-                        dst = uc_of[t][:, qk * H + BH * b : qk * H + BH * (b + 1), :]
-                        if qk:
-                            nc.scalar.activation(out=dst, in_=u[:, :, 0:NS], func=COPY, scale=K_SCALE)
-                        else:
-                            nc.scalar.copy(out=dst, in_=u[:, :, 0:NS])
-                    if t and NS:
-                        i = qk * NB + b
-                        for j in range(2 * NS * i // 8, 2 * NS * (i + 1) // 8):
-                            c, a = divmod(j, 2)
-                            k = 2 * (t - 1) + a
-                            nc.scalar.activation(
-                                out=ms_of[t - 1][:, a, c, :], in_=uc_of[t - 1][:, :, c], func=COPY, scale=tabf[:, k, c : c + 1]
-                            )
                     shape = [P, BH, 2, w]
                     in0 = u[:, :, ns:].unsqueeze(2).to_broadcast(shape)
                     in1 = (tabk if qk else tab)[:, t, :, ns:].unsqueeze(1).to_broadcast(shape)
@@ -202,12 +173,9 @@ def tile_multiscaleretention_pa_kernel(tc, x_words, x_scales, sin, cos, Wq_words
                     elif (2 * t + qk) not in V_UNITS and b % 2:
                         add(nc.gpsimd, m, res, BH * (b - 1), BH * (b + 1), ns)
             if t == 0:
-                nc.scalar.copy(out=tabf[:], in_=tab[:].rearrange("p t a c -> p (t a) c")[:, :, 0:NS])
                 scale_table(1, TT)
             if t:
                 for qk in range(2):
-                    if NS:
-                        add_s(nc.gpsimd, ms_of[t - 1], res_of[t - 1, qk], qk)
                     if 2 * (t - 1) + qk not in V_UNITS:
                         store(t - 1, qk, res_of[t - 1, qk], 0, H)
         for u in range(2 * (TT - 1), 2 * TT):

@@ -18,16 +18,11 @@ TT = T // P
 BH = 2
 BC = BH * KD
 NB = H // BH
+HALF = H // 2
 K_SCALE = KD ** -0.5
-NS = 0
-V_UNITS = (13, 14, 15)
+V_HALVES = ((14, 1), (15, 0), (15, 1))
 
 FLOPS = 2 * T * E * (2 * E) + 3 * T * 2 * E
-
-
-def pairs(ap, swap):
-    v = ap.rearrange("p h (i two) -> p h i two", two=2)
-    return v[:, :, :, ::-1] if swap else v
 
 
 def tile_multiscaleretention_pa_kernel(tc, x_words, x_scales, sin, cos, Wq_words, Wq_scales, Wk_words, Wk_scales, out_0, out_1):
@@ -58,13 +53,16 @@ def tile_multiscaleretention_pa_kernel(tc, x_words, x_scales, sin, cos, Wq_words
                     in_=scales[:, 4 * q : 4 * q + 4, c0 : c0 + cols].rearrange("g r n -> r g n").bitcast(I32),
                 )
 
-        tab = keep.tile([P, TT, 2, KD], BF16, name="tab")
-        sraw = keep.tile([P, TT, KD], BF16, name="sraw")
+        cos_q = keep.tile([P, TT, KD], BF16, name="cos_q")
+        sin_q = keep.tile([P, TT, KD], BF16, name="sin_q")
+        sin_raw = keep.tile([P, TT, KD], BF16, name="sin_raw")
+        cos_k = keep.tile([P, TT, KD], F32, name="cos_k")
+        sin_k = keep.tile([P, TT, KD], F32, name="sin_k")
         sgn = keep.tile([P, 2], BF16, name="sgn")
-        nc.gpsimd.dma_start(out=sraw[:], in_=sin.rearrange("(t p) c -> p t c", p=P))
-        nc.gpsimd.dma_start(out=tab[:, :, 0, :], in_=cos.rearrange("(t p) c -> p t c", p=P))
-        nc.gpsimd.memset(sgn[:, 0:1], 1.0)
-        nc.gpsimd.memset(sgn[:, 1:2], -1.0)
+        nc.gpsimd.dma_start(out=sin_raw[:], in_=sin.rearrange("(t p) c -> p t c", p=P))
+        nc.gpsimd.dma_start(out=cos_q[:], in_=cos.rearrange("(t p) c -> p t c", p=P))
+        nc.gpsimd.memset(sgn[:, 0:1], -1.0)
+        nc.gpsimd.memset(sgn[:, 1:2], 1.0)
 
         xs = plane_tile("xs", T)
         wqs_a = plane_tile("wqs_a", 2 * BC)
@@ -85,25 +83,20 @@ def tile_multiscaleretention_pa_kernel(tc, x_words, x_scales, sin, cos, Wq_words
         load_plane(wks, Wk_scales, 0, E)
         load_codes(xr, x_words, P, T - P)
 
-        sgn_b = sgn[:].unsqueeze(1)
         for t0, t1 in ((0, 1), (1, TT)):
             nc.gpsimd.tensor_tensor(
-                out=pairs(tab[:, t0:t1, 1, :], False),
-                in0=pairs(sraw[:, t0:t1, :], True),
-                in1=sgn_b.unsqueeze(1).to_broadcast([P, t1 - t0, KD // 2, 2]),
+                out=sin_q[:, t0:t1].rearrange("p t (i two) -> p (t i) two", two=2),
+                in0=sin_raw[:, t0:t1].rearrange("p t (i two) -> p (t i) two", two=2),
+                in1=sgn[:].unsqueeze(1).to_broadcast([P, (t1 - t0) * KD // 2, 2]),
                 op=MULT,
             )
-        tabk = keep.tile([P, TT, 2, KD], F32, name="tabk")
 
-        def scale_table(t0, t1):
-            nc.scalar.activation(
-                out=tabk[:, t0:t1].rearrange("p t a c -> p (t a c)"),
-                in_=tab[:, t0:t1].rearrange("p t a c -> p (t a c)"),
-                func=COPY,
-                scale=K_SCALE,
-            )
+        def scale_tables(t0, t1):
+            nc.scalar.activation(out=cos_k[:, t0:t1], in_=cos_q[:, t0:t1], func=COPY, scale=K_SCALE)
+            nc.scalar.activation(out=sin_k[:, t0:t1], in_=sin_q[:, t0:t1], func=COPY, scale=K_SCALE)
 
-        scale_table(0, 1)
+        scale_tables(0, 1)
+        scale_tables(1, TT)
 
         def x_of(t):
             return (x0, 0) if t == 0 else (xr, (t - 1) * P)
@@ -135,55 +128,50 @@ def tile_multiscaleretention_pa_kernel(tc, x_words, x_scales, sin, cos, Wq_words
                         start=(g == 0),
                         stop=(g == G - 1),
                     )
-            return ps[:].rearrange("p (h c) -> p h c", h=BH)
+            return ps
 
-        def add(engine, m, res, h0, h1, ns):
-            engine.tensor_tensor(
-                out=pairs(res[:, h0:h1, ns:], False),
-                in0=pairs(m[:, h0:h1, 0, :], False),
-                in1=pairs(m[:, h0:h1, 1, :], True),
-                op=ADD,
-            )
-
+        def add(engine, m, res, h0, h1):
+            engine.tensor_tensor(out=res[:, h0:h1], in0=m[:, 0, h0:h1], in1=m[:, 1, h0:h1], op=ADD)
 
         def store(t, qk, res, h0, h1):
             nc.sync.dma_start(
                 out=outs[qk][0, h0:h1, t * P : (t + 1) * P, :].rearrange("h t c -> t h c"), in_=res[:, h0:h1, :]
             )
 
-        m_of = {}
-        res_of = {}
+        late = []
         for t in range(TT):
-            ns = NS if t < TT - 1 else 0
-            w = KD - ns
             for qk in range(2):
-                m = prods.tile([P, H, 2, w], F32, name="m")
+                cos_t = (cos_k if qk else cos_q)[:, t, :].unsqueeze(1)
+                sin_t = (sin_k if qk else sin_q)[:, t, :].rearrange("p (i two) -> p i two", two=2).unsqueeze(1)
+                m = prods.tile([P, 2, H, KD], F32, name="m")
                 res = results.tile([P, H, KD], F32, name="res")
-                m_of[t, qk] = m
-                res_of[t, qk] = res
                 for b in range(NB):
-                    u = multiply(t, qk, b)
+                    ps = multiply(t, qk, b)
                     hs = slice(BH * b, BH * (b + 1))
-                    shape = [P, BH, 2, w]
-                    in0 = u[:, :, ns:].unsqueeze(2).to_broadcast(shape)
-                    in1 = (tabk if qk else tab)[:, t, :, ns:].unsqueeze(1).to_broadcast(shape)
-                    nc.vector.tensor_tensor(out=m[:, hs], in0=in0, in1=in1, op=MULT)
+                    nc.vector.tensor_tensor(
+                        out=m[:, 0, hs],
+                        in0=ps[:].rearrange("p (h c) -> p h c", h=BH),
+                        in1=cos_t.to_broadcast([P, BH, KD]),
+                        op=MULT,
+                    )
+                    nc.vector.tensor_tensor(
+                        out=m[:, 1, hs].rearrange("p h (i two) -> p h i two", two=2),
+                        in0=ps[:].rearrange("p (h i two) -> p h i two", h=BH, two=2)[:, :, :, ::-1],
+                        in1=sin_t.to_broadcast([P, BH, KD // 2, 2]),
+                        op=MULT,
+                    )
                     if t == 0 and qk == 0:
-                        add(nc.gpsimd, m, res, BH * b, BH * (b + 1), ns)
-                    elif (2 * t + qk) not in V_UNITS and b % 2:
-                        add(nc.gpsimd, m, res, BH * (b - 1), BH * (b + 1), ns)
-            if t == 0:
-                scale_table(1, TT)
-            if t:
-                for qk in range(2):
-                    if 2 * (t - 1) + qk not in V_UNITS:
-                        store(t - 1, qk, res_of[t - 1, qk], 0, H)
-        for u in range(2 * (TT - 1), 2 * TT):
-            if u not in V_UNITS:
-                store(u // 2, u % 2, res_of[divmod(u, 2)], 0, H)
-        for u in V_UNITS:
-            t, qk = divmod(u, 2)
-            ns = NS if t < TT - 1 else 0
-            for h0 in (0, H // 2):
-                add(nc.vector, m_of[t, qk], res_of[t, qk], h0, h0 + H // 2, ns)
-                store(t, qk, res_of[t, qk], h0, h0 + H // 2)
+                        add(nc.gpsimd, m, res, BH * b, BH * (b + 1))
+                        if b % 2:
+                            store(t, qk, res, BH * (b - 1), BH * (b + 1))
+                    elif b % 2:
+                        half = b // 2
+                        h0 = HALF * half
+                        if (2 * t + qk, half) in V_HALVES:
+                            late.append((t, qk, m, res, h0))
+                        else:
+                            add(nc.gpsimd, m, res, h0, h0 + HALF)
+                            store(t, qk, res, h0, h0 + HALF)
+        for t, qk, m, res, h0 in late:
+            add(nc.vector, m, res, h0, h0 + HALF)
+            store(t, qk, res, h0, h0 + HALF)

@@ -1,6 +1,7 @@
 from contextlib import ExitStack
 
 import concourse.mybir as mybir
+from concourse.masks import make_identity
 
 F32 = mybir.dt.float32
 BF16 = mybir.dt.bfloat16
@@ -12,166 +13,222 @@ MULT = mybir.AluOpType.mult
 ADD = mybir.AluOpType.add
 
 P = 128
-T, E, H, KD = 1024, 1536, 8, 192
-G = E // 512
-TT = T // P
-BH = 2
-BC = BH * KD
-NB = H // BH
-HALF = H // 2
-K_SCALE = KD ** -0.5
-V_HALVES = ((14, 1), (15, 0), (15, 1))
+TOKENS, FEATURES = 1024, 1536
+HEADS, WIDTH = 8, 192
+CHANNELS = HEADS * WIDTH
+HALF = CHANNELS // 2
+PASSES = FEATURES // 512
+TILES = TOKENS // P
+UNITS = 2 * TILES
+BANK = 512
+BANKS = CHANNELS // BANK
+K_FACTOR = WIDTH**-0.5
 
-FLOPS = 2 * T * E * (2 * E) + 3 * T * 2 * E
+X_PARTS = ((0, 128), (128, 256), (256, 512), (512, 1024))
+X_EARLY = 256
+EARLY_TILES = 2
+ROW_PARTS = ((0, 128), (128, WIDTH))
+
+FIRST_SUMS = ((0, 0, 384), (1, 384, 960), (2, 960, 1536))
+SUMS = ((1, 0, HALF), (2, HALF, CHANNELS))
+LAST_SUMS = ((0, 0, 384), (1, 384, HALF), (2, HALF, 1152), (2, 1152, CHANNELS))
+TENSOR_SUM_UNITS = (3, 6, 9)
+SUM_DELAY = 4
+TENSOR_SUM = 384
+
+FLOPS = 2 * TOKENS * FEATURES * (2 * CHANNELS) + 3 * TOKENS * (2 * CHANNELS)
 
 
-def tile_multiscaleretention_pa_kernel(tc, x_words, x_scales, sin, cos, Wq_words, Wq_scales, Wk_words, Wk_scales, out_0, out_1):
+def pairs(ap):
+    return ap.rearrange("p (i two) -> p i two", two=2)
+
+
+def tile_multiscaleretention_pa_kernel(
+    tc, x_words, x_scales, sin, cos, Wq_words, Wq_scales, Wk_words, Wk_scales, out_0, out_1
+):
     nc = tc.nc
     outs = (out_0, out_1)
+
     with ExitStack() as ctx:
         keep = ctx.enter_context(tc.tile_pool(name="keep", bufs=1))
-        prods = ctx.enter_context(tc.tile_pool(name="prods", bufs=8))
-        results = ctx.enter_context(tc.tile_pool(name="results", bufs=8))
+        tables = ctx.enter_context(tc.tile_pool(name="tables", bufs=2))
+        products = ctx.enter_context(tc.tile_pool(name="products", bufs=7))
+        results = ctx.enter_context(tc.tile_pool(name="results", bufs=7))
         psum = ctx.enter_context(tc.psum_pool(name="psum", bufs=8))
         ctx.enter_context(tc.manual_schedule())
 
-        def codes_tile(name, cols):
-            return keep.tile([P, G, 2 * cols], U8, name=name, align_bytes=64)
+        def codes_tile(name, columns):
+            return keep.tile([P, PASSES, 2 * columns], U8, name=name, align_bytes=64)
 
-        def plane_tile(name, cols):
-            plane = keep.tile([P, G, cols], U8, name=name, align_bytes=64)
-            nc.vector.memset(plane[:].rearrange("p g n -> p (g n)").bitcast(I32), 0)
-            return plane
+        def load_codes(tile, words, first, columns):
+            nc.sync.dma_start(
+                out=tile[:].bitcast(I32),
+                in_=words[:, :, 2 * first : 2 * (first + columns)].rearrange("g p n -> p g n").bitcast(I32),
+            )
 
-        def load_codes(tile, words, c0, cols):
-            nc.sync.dma_start(out=tile[:].bitcast(I32), in_=words[:, :, 2 * c0 : 2 * (c0 + cols)].rearrange("g p n -> p g n").bitcast(I32))
+        def plane_tile(name, columns):
+            planes = keep.tile([P, PASSES, columns], U8, name=name, align_bytes=64)
+            nc.vector.memset(planes[:].rearrange("p g n -> p (g n)").bitcast(I32), 0)
+            return planes
 
-        def load_plane(tile, scales, c0, cols):
+        def load_planes(planes, scales, first, columns):
             for q in range(4):
                 nc.sync.dma_start(
-                    out=tile[32 * q : 32 * q + 4, :, :].bitcast(I32),
-                    in_=scales[:, 4 * q : 4 * q + 4, c0 : c0 + cols].rearrange("g r n -> r g n").bitcast(I32),
+                    out=planes[32 * q : 32 * q + 4, :, :].bitcast(I32),
+                    in_=scales[:, 4 * q : 4 * q + 4, first : first + columns].rearrange("g r n -> r g n").bitcast(I32),
                 )
 
-        cos_q = keep.tile([P, TT, KD], BF16, name="cos_q")
-        sin_q = keep.tile([P, TT, KD], BF16, name="sin_q")
-        sin_raw = keep.tile([P, TT, KD], BF16, name="sin_raw")
-        cos_k = keep.tile([P, TT, KD], F32, name="cos_k")
-        sin_k = keep.tile([P, TT, KD], F32, name="sin_k")
-        sgn = keep.tile([P, 2], BF16, name="sgn")
-        nc.gpsimd.dma_start(out=sin_raw[:], in_=sin.rearrange("(t p) c -> p t c", p=P))
-        nc.gpsimd.dma_start(out=cos_q[:], in_=cos.rearrange("(t p) c -> p t c", p=P))
-        nc.gpsimd.memset(sgn[:, 0:1], -1.0)
-        nc.gpsimd.memset(sgn[:, 1:2], 1.0)
+        cos_raw = keep.tile([P, TILES, WIDTH], BF16, name="cos_raw")
+        sin_raw = keep.tile([P, TILES, WIDTH], BF16, name="sin_raw")
+        sin_signed = keep.tile([P, TILES, WIDTH], BF16, name="sin_signed")
 
-        xs = plane_tile("xs", T)
-        wqs_a = plane_tile("wqs_a", 2 * BC)
-        wqs_b = plane_tile("wqs_b", 2 * BC)
-        wks = plane_tile("wks", E)
-        x0 = codes_tile("x0", P)
-        xr = codes_tile("xr", T - P)
-        wq_a = codes_tile("wq_a", BC)
-        wq_b = codes_tile("wq_b", E - BC)
-        wk = codes_tile("wk", E)
-        load_codes(x0, x_words, 0, P)
-        load_codes(wq_a, Wq_words, 0, BC)
-        load_plane(xs, x_scales, 0, T)
-        load_plane(wqs_a, Wq_scales, 0, 2 * BC)
-        load_codes(wq_b, Wq_words, BC, E - BC)
-        load_plane(wqs_b, Wq_scales, 2 * BC, 2 * BC)
-        load_codes(wk, Wk_words, 0, E)
-        load_plane(wks, Wk_scales, 0, E)
-        load_codes(xr, x_words, P, T - P)
+        def load_tables(queue, first_tile, end_tile, first, end):
+            for raw, table in ((cos_raw, cos), (sin_raw, sin)):
+                queue.dma_start(
+                    out=raw[:, first_tile:end_tile, first:end],
+                    in_=table.rearrange("(t p) c -> p t c", p=P)[:, first_tile:end_tile, first:end],
+                )
 
-        for t0, t1 in ((0, 1), (1, TT)):
-            nc.gpsimd.tensor_tensor(
-                out=sin_q[:, t0:t1].rearrange("p t (i two) -> p (t i) two", two=2),
-                in0=sin_raw[:, t0:t1].rearrange("p t (i two) -> p (t i) two", two=2),
-                in1=sgn[:].unsqueeze(1).to_broadcast([P, (t1 - t0) * KD // 2, 2]),
-                op=MULT,
+        load_tables(nc.gpsimd, 0, EARLY_TILES, 0, WIDTH)
+        identity = keep.tile([P, P], F32, name="identity")
+        make_identity(nc, identity[:])
+
+        x_planes_early = plane_tile("x_planes_early", X_EARLY)
+        wq_planes = plane_tile("wq_planes", CHANNELS)
+        wk_planes = plane_tile("wk_planes", CHANNELS)
+        x_planes_late = plane_tile("x_planes_late", TOKENS - X_EARLY)
+        x_codes = [codes_tile("x_codes" + str(first), end - first) for first, end in X_PARTS]
+        wq_codes = [codes_tile("wq_codes" + str(bank), BANK) for bank in range(BANKS)]
+        wk_codes = [codes_tile("wk_codes" + str(bank), BANK) for bank in range(BANKS)]
+
+        def load_x(part):
+            first, end = X_PARTS[part]
+            load_codes(x_codes[part], x_words, first, end - first)
+
+        load_x(0)
+        load_codes(wq_codes[0], Wq_words, 0, BANK)
+        load_planes(x_planes_early, x_scales, 0, X_EARLY)
+        load_planes(wq_planes, Wq_scales, 0, CHANNELS)
+        load_codes(wq_codes[1], Wq_words, BANK, BANK)
+        load_codes(wq_codes[2], Wq_words, 2 * BANK, BANK)
+        load_planes(wk_planes, Wk_scales, 0, CHANNELS)
+        for bank in range(BANKS):
+            load_codes(wk_codes[bank], Wk_words, bank * BANK, BANK)
+        load_x(1)
+        load_planes(x_planes_late, x_scales, X_EARLY, TOKENS - X_EARLY)
+        load_x(2)
+        for first, end in ROW_PARTS:
+            load_tables(nc.sync, EARLY_TILES, TILES, first, end)
+        load_x(3)
+
+        def make_tables(t):
+            table = tables.tile([P, 2, 2, 4, WIDTH], F32, name="table")
+
+            def repeat(qk, which, raw):
+                nc.scalar.activation(
+                    out=table[:, qk, which],
+                    in_=raw[:, t, :].unsqueeze(1).to_broadcast([P, 4, WIDTH]),
+                    func=COPY,
+                    scale=K_FACTOR if qk else 1.0,
+                )
+
+            repeat(0, 0, cos_raw)
+            for parity, sign in enumerate((-1.0, 1.0)):
+                nc.scalar.activation(
+                    out=pairs(sin_signed[:, t, :])[:, :, parity],
+                    in_=pairs(sin_raw[:, t, :])[:, :, parity],
+                    func=COPY,
+                    scale=sign,
+                )
+            repeat(0, 1, sin_signed)
+            repeat(1, 0, cos_raw)
+            repeat(1, 1, sin_signed)
+            return table
+
+        def project(t, qk, bank):
+            part = [end > t * P for first, end in X_PARTS].index(True)
+            x_first = t * P - X_PARTS[part][0]
+            early = (t + 1) * P <= X_EARLY
+            x_planes = x_planes_early if early else x_planes_late
+            plane_first = t * P - (0 if early else X_EARLY)
+            w_codes = (wk_codes if qk else wq_codes)[bank]
+            w_planes = wk_planes if qk else wq_planes
+            u = psum.tile([P, BANK], F32, name="bank")
+            for g in range(PASSES):
+                nc.tensor.matmul_mx(
+                    out=u[:],
+                    lhsT=x_codes[part][:, g, 2 * x_first : 2 * (x_first + P)].bitcast(FP4X4),
+                    lhsT_scale=x_planes[:, g, plane_first : plane_first + P],
+                    rhs=w_codes[:, g, :].bitcast(FP4X4),
+                    rhs_scale=w_planes[:, g, bank * BANK : (bank + 1) * BANK],
+                    start=(g == 0),
+                    stop=(g == PASSES - 1),
+                )
+            return u
+
+        def rotate_bank(u, table, product, bank):
+            channels = slice(bank * BANK, (bank + 1) * BANK)
+            first = bank * BANK % WIDTH
+            cos_bank = table[:, 0, first : first + BANK]
+            sin_bank = table[:, 1, first : first + BANK]
+            nc.vector.tensor_tensor(out=product[:, 0, channels], in0=u[:], in1=cos_bank, op=MULT)
+            nc.vector.tensor_tensor(
+                out=pairs(product[:, 1, channels]), in0=pairs(u[:])[:, :, ::-1], in1=pairs(sin_bank), op=MULT
             )
 
-        def scale_tables(t0, t1):
-            nc.scalar.activation(out=cos_k[:, t0:t1], in_=cos_q[:, t0:t1], func=COPY, scale=K_SCALE)
-            nc.scalar.activation(out=sin_k[:, t0:t1], in_=sin_q[:, t0:t1], func=COPY, scale=K_SCALE)
+        def store(unit, result, first, end):
+            t, qk = divmod(unit, 2)
+            heads = slice(first // WIDTH, end // WIDTH)
+            rows = result[:].rearrange("p (h c) -> p h c", c=WIDTH)
+            for c0, c1 in ROW_PARTS:
+                nc.sync.dma_start(
+                    out=outs[qk][0, heads, t * P : (t + 1) * P, c0:c1].rearrange("h t c -> t h c"),
+                    in_=rows[:, heads, c0:c1],
+                )
 
-        scale_tables(0, 1)
-        scale_tables(1, TT)
-
-        def x_of(t):
-            return (x0, 0) if t == 0 else (xr, (t - 1) * P)
-
-        def w_codes(qk, c):
-            if qk:
-                return wk, c
-            return (wq_a, c) if c < BC else (wq_b, c - BC)
-
-        def w_plane(qk, c):
-            if qk:
-                return wks, c
-            return (wqs_a, c) if c < 2 * BC else (wqs_b, c - 2 * BC)
-
-        def multiply(t, qk, b):
-            ps = psum.tile([P, BC], F32, name="ps")
-            xt, xc = x_of(t)
-            for n0, n in ((0, 256), (256, 128)):
-                c = b * BC + n0
-                wt, wc = w_codes(qk, c)
-                st, sc = w_plane(qk, c)
-                for g in range(G):
-                    nc.tensor.matmul_mx(
-                        out=ps[:, n0 : n0 + n],
-                        lhsT=xt[:, g, 2 * xc : 2 * (xc + P)].bitcast(FP4X4),
-                        lhsT_scale=xs[:, g, t * P : (t + 1) * P],
-                        rhs=wt[:, g, 2 * wc : 2 * (wc + n)].bitcast(FP4X4),
-                        rhs_scale=st[:, g, sc : sc + n],
-                        start=(g == 0),
-                        stop=(g == G - 1),
-                    )
-            return ps
-
-        def add(engine, m, res, h0, h1):
-            engine.tensor_tensor(out=res[:, h0:h1], in0=m[:, 0, h0:h1], in1=m[:, 1, h0:h1], op=ADD)
-
-        def store(t, qk, res, h0, h1):
-            nc.sync.dma_start(
-                out=outs[qk][0, h0:h1, t * P : (t + 1) * P, :].rearrange("h t c -> t h c"), in_=res[:, h0:h1, :]
+        def add(engine, unit, product, result, first, end):
+            engine.tensor_tensor(
+                out=result[:, first:end], in0=product[:, 0, first:end], in1=product[:, 1, first:end], op=ADD
             )
+            store(unit, result, first, end)
 
-        late = []
-        for t in range(TT):
-            for qk in range(2):
-                cos_t = (cos_k if qk else cos_q)[:, t, :].unsqueeze(1)
-                sin_t = (sin_k if qk else sin_q)[:, t, :].rearrange("p (i two) -> p i two", two=2).unsqueeze(1)
-                m = prods.tile([P, 2, H, KD], F32, name="m")
-                res = results.tile([P, H, KD], F32, name="res")
-                for b in range(NB):
-                    ps = multiply(t, qk, b)
-                    hs = slice(BH * b, BH * (b + 1))
-                    nc.vector.tensor_tensor(
-                        out=m[:, 0, hs],
-                        in0=ps[:].rearrange("p (h c) -> p h c", h=BH),
-                        in1=cos_t.to_broadcast([P, BH, KD]),
-                        op=MULT,
+        def add_on_tensor(unit, product, result, first, end):
+            for c in range(first, end, TENSOR_SUM):
+                total = psum.tile([P, BANK], F32, name="bank")
+                for which in range(2):
+                    nc.tensor.matmul(
+                        total[:, 0:TENSOR_SUM],
+                        identity[:],
+                        product[:, which, c : c + TENSOR_SUM],
+                        start=(which == 0),
+                        stop=(which == 1),
                     )
-                    nc.vector.tensor_tensor(
-                        out=m[:, 1, hs].rearrange("p h (i two) -> p h i two", two=2),
-                        in0=ps[:].rearrange("p (h i two) -> p h i two", h=BH, two=2)[:, :, :, ::-1],
-                        in1=sin_t.to_broadcast([P, BH, KD // 2, 2]),
-                        op=MULT,
-                    )
-                    if t == 0 and qk == 0:
-                        add(nc.gpsimd, m, res, BH * b, BH * (b + 1))
-                        if b % 2:
-                            store(t, qk, res, BH * (b - 1), BH * (b + 1))
-                    elif b % 2:
-                        half = b // 2
-                        h0 = HALF * half
-                        if (2 * t + qk, half) in V_HALVES:
-                            late.append((t, qk, m, res, h0))
-                        else:
-                            add(nc.gpsimd, m, res, h0, h0 + HALF)
-                            store(t, qk, res, h0, h0 + HALF)
-        for t, qk, m, res, h0 in late:
-            add(nc.vector, m, res, h0, h0 + HALF)
-            store(t, qk, res, h0, h0 + HALF)
+                nc.scalar.copy(out=result[:, c : c + TENSOR_SUM], in_=total[:, 0:TENSOR_SUM])
+            store(unit, result, first, end)
+
+        delayed = {}
+        table, next_table = None, make_tables(0)
+        for unit in range(UNITS):
+            t, qk = divmod(unit, 2)
+            if qk == 0:
+                table = next_table
+                if t + 1 < TILES:
+                    next_table = make_tables(t + 1)
+            for job in delayed.get(unit, ()):
+                add_on_tensor(*job)
+            product = products.tile([P, 2, CHANNELS], F32, name="product")
+            result = results.tile([P, CHANNELS], F32, name="result", align_bytes=256)
+            sums = FIRST_SUMS if unit == 0 else LAST_SUMS if unit == UNITS - 1 else SUMS
+            for bank in range(BANKS):
+                u = project(t, qk, bank)
+                rotate_bank(u, table[:, qk].rearrange("p a r c -> p a (r c)"), product, bank)
+                for last_bank, first, end in sums:
+                    if last_bank != bank:
+                        continue
+                    job = (unit, product, result, first, end)
+                    if unit in TENSOR_SUM_UNITS and first == HALF:
+                        delayed[unit + SUM_DELAY] = (job,)
+                    elif unit == UNITS - 1 and first >= HALF:
+                        add(nc.vector, *job)
+                    else:
+                        add(nc.gpsimd, *job)

from contextlib import ExitStack

import concourse.mybir as mybir
from concourse.masks import make_identity

F32 = mybir.dt.float32
BF16 = mybir.dt.bfloat16
I32 = mybir.dt.int32
U8 = mybir.dt.uint8
FP4X4 = mybir.dt.float4_e2m1fn_x4
COPY = mybir.ActivationFunctionType.Copy
MULT = mybir.AluOpType.mult
ADD = mybir.AluOpType.add

P = 128
TOKENS, FEATURES = 1024, 1536
HEADS, WIDTH = 8, 192
CHANNELS = HEADS * WIDTH
HALF = CHANNELS // 2
PASSES = FEATURES // 512
TILES = TOKENS // P
UNITS = 2 * TILES
BANK = 512
BANKS = CHANNELS // BANK
K_FACTOR = WIDTH**-0.5

X_PARTS = ((0, 128), (128, 256), (256, 512), (512, 1024))
X_EARLY = 256
EARLY_TILES = 2
ROW_PARTS = ((0, 128), (128, WIDTH))

FIRST_SUMS = ((0, 0, 384), (1, 384, 960), (2, 960, 1536))
SUMS = ((1, 0, HALF), (2, HALF, CHANNELS))
LAST_SUMS = ((0, 0, 384), (1, 384, HALF), (2, HALF, 1152), (2, 1152, CHANNELS))
TENSOR_SUM_UNITS = (3, 6, 9)
SUM_DELAY = 4
TENSOR_SUM = 384

FLOPS = 2 * TOKENS * FEATURES * (2 * CHANNELS) + 3 * TOKENS * (2 * CHANNELS)


def pairs(ap):
    return ap.rearrange("p (i two) -> p i two", two=2)


def tile_multiscaleretention_pa_kernel(
    tc, x_words, x_scales, sin, cos, Wq_words, Wq_scales, Wk_words, Wk_scales, out_0, out_1
):
    nc = tc.nc
    outs = (out_0, out_1)

    with ExitStack() as ctx:
        keep = ctx.enter_context(tc.tile_pool(name="keep", bufs=1))
        tables = ctx.enter_context(tc.tile_pool(name="tables", bufs=2))
        products = ctx.enter_context(tc.tile_pool(name="products", bufs=7))
        results = ctx.enter_context(tc.tile_pool(name="results", bufs=7))
        psum = ctx.enter_context(tc.psum_pool(name="psum", bufs=8))
        ctx.enter_context(tc.manual_schedule())

        def codes_tile(name, columns):
            return keep.tile([P, PASSES, 2 * columns], U8, name=name, align_bytes=64)

        def load_codes(tile, words, first, columns):
            nc.sync.dma_start(
                out=tile[:].bitcast(I32),
                in_=words[:, :, 2 * first : 2 * (first + columns)].rearrange("g p n -> p g n").bitcast(I32),
            )

        def plane_tile(name, columns):
            planes = keep.tile([P, PASSES, columns], U8, name=name, align_bytes=64)
            nc.vector.memset(planes[:].rearrange("p g n -> p (g n)").bitcast(I32), 0)
            return planes

        def load_planes(planes, scales, first, columns):
            for q in range(4):
                nc.sync.dma_start(
                    out=planes[32 * q : 32 * q + 4, :, :].bitcast(I32),
                    in_=scales[:, 4 * q : 4 * q + 4, first : first + columns].rearrange("g r n -> r g n").bitcast(I32),
                )

        cos_raw = keep.tile([P, TILES, WIDTH], BF16, name="cos_raw")
        sin_raw = keep.tile([P, TILES, WIDTH], BF16, name="sin_raw")
        sin_signed = keep.tile([P, TILES, WIDTH], BF16, name="sin_signed")

        def load_tables(queue, first_tile, end_tile, first, end):
            for raw, table in ((cos_raw, cos), (sin_raw, sin)):
                queue.dma_start(
                    out=raw[:, first_tile:end_tile, first:end],
                    in_=table.rearrange("(t p) c -> p t c", p=P)[:, first_tile:end_tile, first:end],
                )

        load_tables(nc.gpsimd, 0, EARLY_TILES, 0, WIDTH)
        identity = keep.tile([P, P], F32, name="identity")
        make_identity(nc, identity[:])

        x_planes_early = plane_tile("x_planes_early", X_EARLY)
        wq_planes = plane_tile("wq_planes", CHANNELS)
        wk_planes = plane_tile("wk_planes", CHANNELS)
        x_planes_late = plane_tile("x_planes_late", TOKENS - X_EARLY)
        x_codes = [codes_tile("x_codes" + str(first), end - first) for first, end in X_PARTS]
        wq_codes = [codes_tile("wq_codes" + str(bank), BANK) for bank in range(BANKS)]
        wk_codes = [codes_tile("wk_codes" + str(bank), BANK) for bank in range(BANKS)]

        def load_x(part):
            first, end = X_PARTS[part]
            load_codes(x_codes[part], x_words, first, end - first)

        load_x(0)
        load_codes(wq_codes[0], Wq_words, 0, BANK)
        load_planes(x_planes_early, x_scales, 0, X_EARLY)
        load_planes(wq_planes, Wq_scales, 0, CHANNELS)
        load_codes(wq_codes[1], Wq_words, BANK, BANK)
        load_codes(wq_codes[2], Wq_words, 2 * BANK, BANK)
        load_planes(wk_planes, Wk_scales, 0, CHANNELS)
        for bank in range(BANKS):
            load_codes(wk_codes[bank], Wk_words, bank * BANK, BANK)
        load_x(1)
        load_planes(x_planes_late, x_scales, X_EARLY, TOKENS - X_EARLY)
        load_x(2)
        for first, end in ROW_PARTS:
            load_tables(nc.sync, EARLY_TILES, TILES, first, end)
        load_x(3)

        def make_tables(t):
            table = tables.tile([P, 2, 2, 4, WIDTH], F32, name="table")

            def repeat(qk, which, raw):
                nc.scalar.activation(
                    out=table[:, qk, which],
                    in_=raw[:, t, :].unsqueeze(1).to_broadcast([P, 4, WIDTH]),
                    func=COPY,
                    scale=K_FACTOR if qk else 1.0,
                )

            repeat(0, 0, cos_raw)
            for parity, sign in enumerate((-1.0, 1.0)):
                nc.scalar.activation(
                    out=pairs(sin_signed[:, t, :])[:, :, parity],
                    in_=pairs(sin_raw[:, t, :])[:, :, parity],
                    func=COPY,
                    scale=sign,
                )
            repeat(0, 1, sin_signed)
            repeat(1, 0, cos_raw)
            repeat(1, 1, sin_signed)
            return table

        def project(t, qk, bank):
            part = [end > t * P for first, end in X_PARTS].index(True)
            x_first = t * P - X_PARTS[part][0]
            early = (t + 1) * P <= X_EARLY
            x_planes = x_planes_early if early else x_planes_late
            plane_first = t * P - (0 if early else X_EARLY)
            w_codes = (wk_codes if qk else wq_codes)[bank]
            w_planes = wk_planes if qk else wq_planes
            u = psum.tile([P, BANK], F32, name="bank")
            for g in range(PASSES):
                nc.tensor.matmul_mx(
                    out=u[:],
                    lhsT=x_codes[part][:, g, 2 * x_first : 2 * (x_first + P)].bitcast(FP4X4),
                    lhsT_scale=x_planes[:, g, plane_first : plane_first + P],
                    rhs=w_codes[:, g, :].bitcast(FP4X4),
                    rhs_scale=w_planes[:, g, bank * BANK : (bank + 1) * BANK],
                    start=(g == 0),
                    stop=(g == PASSES - 1),
                )
            return u

        def rotate_bank(u, table, product, bank):
            channels = slice(bank * BANK, (bank + 1) * BANK)
            first = bank * BANK % WIDTH
            cos_bank = table[:, 0, first : first + BANK]
            sin_bank = table[:, 1, first : first + BANK]
            nc.vector.tensor_tensor(out=product[:, 0, channels], in0=u[:], in1=cos_bank, op=MULT)
            nc.vector.tensor_tensor(
                out=pairs(product[:, 1, channels]), in0=pairs(u[:])[:, :, ::-1], in1=pairs(sin_bank), op=MULT
            )

        def store(unit, result, first, end):
            t, qk = divmod(unit, 2)
            heads = slice(first // WIDTH, end // WIDTH)
            rows = result[:].rearrange("p (h c) -> p h c", c=WIDTH)
            for c0, c1 in ROW_PARTS:
                nc.sync.dma_start(
                    out=outs[qk][0, heads, t * P : (t + 1) * P, c0:c1].rearrange("h t c -> t h c"),
                    in_=rows[:, heads, c0:c1],
                )

        def add(engine, unit, product, result, first, end):
            engine.tensor_tensor(
                out=result[:, first:end], in0=product[:, 0, first:end], in1=product[:, 1, first:end], op=ADD
            )
            store(unit, result, first, end)

        def add_on_tensor(unit, product, result, first, end):
            for c in range(first, end, TENSOR_SUM):
                total = psum.tile([P, BANK], F32, name="bank")
                for which in range(2):
                    nc.tensor.matmul(
                        total[:, 0:TENSOR_SUM],
                        identity[:],
                        product[:, which, c : c + TENSOR_SUM],
                        start=(which == 0),
                        stop=(which == 1),
                    )
                nc.scalar.copy(out=result[:, c : c + TENSOR_SUM], in_=total[:, 0:TENSOR_SUM])
            store(unit, result, first, end)

        delayed = {}
        table, next_table = None, make_tables(0)
        for unit in range(UNITS):
            t, qk = divmod(unit, 2)
            if qk == 0:
                table = next_table
                if t + 1 < TILES:
                    next_table = make_tables(t + 1)
            for job in delayed.get(unit, ()):
                add_on_tensor(*job)
            product = products.tile([P, 2, CHANNELS], F32, name="product")
            result = results.tile([P, CHANNELS], F32, name="result", align_bytes=256)
            sums = FIRST_SUMS if unit == 0 else LAST_SUMS if unit == UNITS - 1 else SUMS
            for bank in range(BANKS):
                u = project(t, qk, bank)
                rotate_bank(u, table[:, qk].rearrange("p a r c -> p a (r c)"), product, bank)
                for last_bank, first, end in sums:
                    if last_bank != bank:
                        continue
                    job = (unit, product, result, first, end)
                    if unit in TENSOR_SUM_UNITS and first == HALF:
                        delayed[unit + SUM_DELAY] = (job,)
                    elif unit == UNITS - 1 and first >= HALF:
                        add(nc.vector, *job)
                    else:
                        add(nc.gpsimd, *job)
